import numpy as np
import ml_dtypes


def mxq(x, axis, fmt="e4m3"):
    dtype, down = {"e4m3": (ml_dtypes.float8_e4m3fn, 7), "e5m2": (ml_dtypes.float8_e5m2, 14)}[fmt]
    v = np.moveaxis(np.asarray(x, np.float32).astype(ml_dtypes.bfloat16).astype(np.float64), axis, -1)
    blocks = v.reshape(v.shape[:-1] + (-1, 32))
    amax = np.abs(blocks).max(-1, keepdims=True)
    byte = np.maximum(np.where(amax > 0, np.frexp(amax)[1] - 1 + 127, 0) - down, 1)
    scale = np.exp2(byte - 127.0)
    codes = (blocks / scale).astype(np.float32).astype(dtype).astype(np.float64)
    return np.moveaxis((codes * scale).reshape(v.shape), -1, axis)


WIDE = False


def mx_kscale(k):
    if not WIDE:
        return np.ones(k)
    levels = np.array([10, -10, 5, -5, 0])
    a = np.random.permutation(np.resize(levels, k // 512 * 4)).reshape(k // 512, 4)
    idx = np.arange(k)
    return np.exp2(a[idx // 512, idx % 128 // 32])


BF16 = ml_dtypes.bfloat16


def bf(x):
    return np.asarray(x, np.float32).astype(BF16)


def f64(x):
    return np.asarray(x).astype(np.float64)


B, S, DIM, N_HEADS, Q_LORA, KV_LORA, NOPE, ROPE, V_HEAD = 4, 1024, 256, 2, 1536, 1024, 128, 64, 256
HV = N_HEADS * V_HEAD


def setup_inputs():
    s, t = mx_kscale(KV_LORA), mx_kscale(HV)
    return {"o_lat": bf(np.random.standard_normal((B, S, N_HEADS, KV_LORA)) * 0.35 * s),
            "w_uv": bf(np.random.standard_normal((N_HEADS, V_HEAD, KV_LORA)) * 2.0 / np.sqrt(KV_LORA) / s * t.reshape(N_HEADS, V_HEAD, 1)),
            "wo": bf(np.random.standard_normal((DIM, HV)) / np.sqrt(HV) / t)}


def reference(o_lat, w_uv, wo):
    ol = mxq(f64(o_lat), 3, "e4m3").transpose(0, 2, 1, 3)
    wv = mxq(f64(w_uv), 2, "e4m3").transpose(0, 2, 1)
    o = ol @ wv[None]
    o = o.transpose(0, 2, 1, 3).reshape(B, S, HV)
    return mxq(o, 2, "e4m3") @ mxq(f64(wo), 1, "e4m3").T

@@ -1,0 +1,184 @@
+from contextlib import ExitStack
+
+import concourse.masks as masks
+import concourse.mybir as mybir
+
+F32 = mybir.dt.float32
+BF16 = mybir.dt.bfloat16
+U32 = mybir.dt.uint32
+U8 = mybir.dt.uint8
+FP8X4 = mybir.dt.float8_e4m3fn_x4
+
+P = 128
+TOKENS = 4 * 1024
+HEADS = 2
+LATENT = 1024
+V_HEAD = 256
+JOINED = HEADS * V_HEAD
+DIM = 256
+
+PACK = 4
+UNIT = 1024
+UNIT_WORDS = UNIT // 2
+UNIT_CODES = UNIT // PACK
+BLOCKS = UNIT_WORDS // P
+PASSES = LATENT // (P * PACK)
+
+TILES = TOKENS // P
+ROUND_TILES = 2
+ROUNDS = TILES // ROUND_TILES
+ROUNDS_AHEAD = 6
+
+FLOPS = 2 * TOKENS * HEADS * V_HEAD * LATENT + 2 * TOKENS * JOINED * DIM
+
+
+def tile_mla_pc_t_kernel(tc, o_lat, w_uv, wo, out):
+    nc = tc.nc
+
+    x_rows = o_lat.rearrange("b (q t) h c -> (b q) (t h c)", t=TILES)
+    out_rows = out.rearrange("b (q t) f -> (b q) (t f)", t=TILES)
+    x_round = ROUND_TILES * HEADS * LATENT
+    out_round = ROUND_TILES * DIM
+
+    with ExitStack() as ctx:
+        keep = ctx.enter_context(tc.tile_pool(name="keep", bufs=1))
+        raw_pool = ctx.enter_context(tc.tile_pool(name="raw", bufs=ROUNDS_AHEAD))
+        per_tile = ctx.enter_context(tc.tile_pool(name="per_tile", bufs=2 * ROUND_TILES))
+        per_round = ctx.enter_context(tc.tile_pool(name="per_round", bufs=2))
+        result_pool = ctx.enter_context(tc.tile_pool(name="result", bufs=4))
+        unit_banks = ctx.enter_context(tc.psum_pool(name="unit_banks", bufs=2 * ROUND_TILES))
+        o_banks = ctx.enter_context(tc.psum_pool(name="o_banks", bufs=2))
+        out_banks = ctx.enter_context(tc.psum_pool(name="out_banks", bufs=2))
+        ctx.enter_context(tc.manual_schedule())
+
+        identity = keep.tile([P, P], F32)
+        masks.make_identity(nc, identity[:])
+
+        def load_round(r):
+            raw = raw_pool.tile([P, x_round], BF16)
+            nc.sync.dma_start(out=raw[:], in_=x_rows[:, r * x_round : (r + 1) * x_round])
+            return raw
+
+        def transpose_units(words, units):
+            grouped = per_tile.tile([P, units * UNIT], BF16, tag="grouped", align_bytes=64)
+            grouped_words = grouped[:].bitcast(F32)
+            for n in range(units):
+                bank = unit_banks.tile([P, UNIT_WORDS], F32)
+                for block in range(BLOCKS):
+                    nc.tensor.transpose(
+                        bank[:, block * P : (block + 1) * P],
+                        words[:, n * UNIT_WORDS + block * P : n * UNIT_WORDS + (block + 1) * P],
+                        identity[:],
+                    )
+                nc.scalar.copy(
+                    out=grouped_words[:, n * UNIT_WORDS : (n + 1) * UNIT_WORDS].rearrange(
+                        "p (g r u) -> p g r u", g=PASSES, u=2
+                    ),
+                    in_=bank[:].rearrange("p (g u r) -> p g r u", g=PASSES, u=2),
+                )
+            return grouped
+
+        def quantise(grouped, codes, scales):
+            nc.vector.quantize_mx(out=codes.bitcast(FP8X4), scales=scales, in_=grouped[:])
+
+        w_raw = keep.tile([P, HEADS * 2 * UNIT], BF16)
+        nc.sync.dma_start(
+            out=w_raw[:].rearrange("q (h f) -> q h f", h=HEADS),
+            in_=w_uv.rearrange("h (q e) c -> q h (e c)", e=2),
+        )
+        wo_raw = keep.tile([P, UNIT], BF16)
+        nc.sync.dma_start(
+            out=wo_raw[:].rearrange("p (a k) -> p a k", a=DIM // P),
+            in_=wo.rearrange("(a p) k -> p a k", p=P),
+        )
+        raw_of = {}
+        for r in range(ROUNDS_AHEAD):
+            raw_of[r] = load_round(r)
+
+        w_codes = keep.tile([P, HEADS * 2 * UNIT_CODES], U32, align_bytes=64)
+        w_scales = keep.tile([P, HEADS * 2 * UNIT_CODES], U8, align_bytes=64)
+        wo_codes = keep.tile([P, DIM], U32, align_bytes=64)
+        wo_scales = keep.tile([P, DIM], U8, align_bytes=64)
+        w_words = w_raw[:].bitcast(F32)
+        for h in range(HEADS):
+            w_grouped = transpose_units(w_words[:, h * 2 * UNIT_WORDS : (h + 1) * 2 * UNIT_WORDS], 2)
+            head_cols = slice(h * 2 * UNIT_CODES, (h + 1) * 2 * UNIT_CODES)
+            quantise(w_grouped, w_codes[:, head_cols], w_scales[:, head_cols])
+        wo_grouped = transpose_units(wo_raw[:].bitcast(F32), 1)
+        quantise(wo_grouped, wo_codes[:], wo_scales[:])
+
+        def stage_1(x_codes, x_scales, o_grouped_tile):
+            o_bank = o_banks.tile([P, PACK * P], F32)
+            for j in range(PACK):
+                h = j // 2
+                for g in range(PASSES):
+                    w_cols = slice((j * PASSES + g) * P, (j * PASSES + g + 1) * P)
+                    x_cols = slice((h * PASSES + g) * P, (h * PASSES + g + 1) * P)
+                    nc.tensor.matmul_mx(
+                        out=o_bank[:, j * P : (j + 1) * P],
+                        lhsT=w_codes[:, w_cols].bitcast(FP8X4),
+                        lhsT_scale=w_scales[:, w_cols],
+                        rhs=x_codes[:, x_cols].bitcast(FP8X4),
+                        rhs_scale=x_scales[:, x_cols],
+                        start=(g == 0),
+                        stop=(g == PASSES - 1),
+                    )
+            nc.vector.tensor_copy(
+                out=o_grouped_tile.rearrange("p (r j) -> p r j", j=PACK),
+                in_=o_bank[:].rearrange("p (j r) -> p r j", j=PACK),
+            )
+
+        def stage_2(r, o_codes, o_scales):
+            out_bank = out_banks.tile([P, out_round], F32)
+            for i in range(ROUND_TILES):
+                nc.tensor.matmul_mx(
+                    out=out_bank[:, i * DIM : (i + 1) * DIM],
+                    lhsT=o_codes[:, i * P : (i + 1) * P].bitcast(FP8X4),
+                    lhsT_scale=o_scales[:, i * P : (i + 1) * P],
+                    rhs=wo_codes[:].bitcast(FP8X4),
+                    rhs_scale=wo_scales[:],
+                    start=True,
+                    stop=True,
+                )
+            result = result_pool.tile([P, out_round], F32)
+            nc.scalar.copy(out=result[:], in_=out_bank[:])
+            nc.sync.dma_start(out=out_rows[:, r * out_round : (r + 1) * out_round], in_=result[:])
+
+        x_quantised = {}
+        o_grouped_of = {}
+        for r in range(ROUNDS + 2):
+            transposing = r < ROUNDS
+            in_stage_1 = 0 <= r - 1 < ROUNDS
+            in_stage_2 = 0 <= r - 2
+
+            if in_stage_2:
+                o_codes = per_round.tile([P, ROUND_TILES * P], U32, align_bytes=64)
+                o_scales = per_round.tile([P, ROUND_TILES * P], U8, align_bytes=64)
+                quantise(o_grouped_of[r - 2], o_codes[:], o_scales[:])
+
+            if transposing:
+                x_words = raw_of[r][:].bitcast(F32)
+                tile_words = HEADS * UNIT_WORDS
+                x_grouped = [
+                    transpose_units(x_words[:, i * tile_words : (i + 1) * tile_words], HEADS)
+                    for i in range(ROUND_TILES)
+                ]
+                if r + ROUNDS_AHEAD < ROUNDS:
+                    raw_of[r + ROUNDS_AHEAD] = load_round(r + ROUNDS_AHEAD)
+                x_quantised[r] = []
+            if in_stage_1:
+                o_grouped = per_round.tile([P, ROUND_TILES * P * PACK], BF16, align_bytes=64)
+                o_grouped_of[r - 1] = o_grouped
+
+            for i in range(ROUND_TILES):
+                if transposing:
+                    x_codes = per_tile.tile([P, HEADS * UNIT_CODES], U32, align_bytes=64)
+                    x_scales = per_tile.tile([P, HEADS * UNIT_CODES], U8, align_bytes=64)
+                    quantise(x_grouped[i], x_codes[:], x_scales[:])
+                    x_quantised[r].append((x_codes, x_scales))
+                if in_stage_1:
+                    codes, scales = x_quantised[r - 1][i]
+                    stage_1(codes, scales, o_grouped[:, i * P * PACK : (i + 1) * P * PACK])
+
+            if in_stage_2:
+                stage_2(r - 2, o_codes, o_scales)

@@ -23,11 +23,13 @@ UNIT_WORDS = UNIT // 2
 UNIT_CODES = UNIT // PACK
 BLOCKS = UNIT_WORDS // P
 PASSES = LATENT // (P * PACK)
+PSUM_BANKS = 8
 
-TILES = TOKENS // P
-ROUND_TILES = 2
-ROUNDS = TILES // ROUND_TILES
-ROUNDS_AHEAD = 6
+PAIR = 2
+PAIRS = TOKENS // (P * PAIR)
+RUN_PAIRS = 2
+RUNS = PAIRS // RUN_PAIRS
+PAIRS_AHEAD = 6
 
 FLOPS = 2 * TOKENS * HEADS * V_HEAD * LATENT + 2 * TOKENS * JOINED * DIM
 
@@ -35,35 +37,27 @@ FLOPS = 2 * TOKENS * HEADS * V_HEAD * LATENT + 2 * TOKENS * JOINED * DIM
 def tile_mla_pc_t_kernel(tc, o_lat, w_uv, wo, out):
     nc = tc.nc
 
-    x_rows = o_lat.rearrange("b (q t) h c -> (b q) (t h c)", t=TILES)
-    out_rows = out.rearrange("b (q t) f -> (b q) (t f)", t=TILES)
-    x_round = ROUND_TILES * HEADS * LATENT
-    out_round = ROUND_TILES * DIM
+    x_rows = o_lat.rearrange("b (q t) h c -> (b q) (t h c)", t=PAIR * PAIRS)
+    out_rows = out.rearrange("b (q t) f -> (b q) (t f)", t=PAIR * PAIRS)
+    x_pair = PAIR * HEADS * LATENT
+    out_pair = PAIR * DIM
 
     with ExitStack() as ctx:
         keep = ctx.enter_context(tc.tile_pool(name="keep", bufs=1))
-        raw_pool = ctx.enter_context(tc.tile_pool(name="raw", bufs=ROUNDS_AHEAD))
-        per_tile = ctx.enter_context(tc.tile_pool(name="per_tile", bufs=2 * ROUND_TILES))
-        per_round = ctx.enter_context(tc.tile_pool(name="per_round", bufs=2))
-        result_pool = ctx.enter_context(tc.tile_pool(name="result", bufs=4))
-        unit_banks = ctx.enter_context(tc.psum_pool(name="unit_banks", bufs=2 * ROUND_TILES))
-        o_banks = ctx.enter_context(tc.psum_pool(name="o_banks", bufs=2))
-        out_banks = ctx.enter_context(tc.psum_pool(name="out_banks", bufs=2))
+        raw_pool = ctx.enter_context(tc.tile_pool(name="raw", bufs=PAIRS_AHEAD))
+        per_tile = ctx.enter_context(tc.tile_pool(name="per_tile", bufs=2 * RUN_PAIRS * PAIR))
+        per_pair = ctx.enter_context(tc.tile_pool(name="per_pair", bufs=2 * RUN_PAIRS))
+        banks = ctx.enter_context(tc.psum_pool(name="banks", bufs=PSUM_BANKS))
         ctx.enter_context(tc.manual_schedule())
 
         identity = keep.tile([P, P], F32)
         masks.make_identity(nc, identity[:])
 
-        def load_round(r):
-            raw = raw_pool.tile([P, x_round], BF16)
-            nc.sync.dma_start(out=raw[:], in_=x_rows[:, r * x_round : (r + 1) * x_round])
-            return raw
-
         def transpose_units(words, units):
             grouped = per_tile.tile([P, units * UNIT], BF16, tag="grouped", align_bytes=64)
             grouped_words = grouped[:].bitcast(F32)
             for n in range(units):
-                bank = unit_banks.tile([P, UNIT_WORDS], F32)
+                bank = banks.tile([P, UNIT_WORDS], F32, tag="bank")
                 for block in range(BLOCKS):
                     nc.tensor.transpose(
                         bank[:, block * P : (block + 1) * P],
@@ -81,104 +75,132 @@ def tile_mla_pc_t_kernel(tc, o_lat, w_uv, wo, out):
         def quantise(grouped, codes, scales):
             nc.vector.quantize_mx(out=codes.bitcast(FP8X4), scales=scales, in_=grouped[:])
 
+        raw_of = {}
+        x_grouped_of = {}
+        x_quantised_of = {}
+        o_grouped_of = {}
+        o_quantised_of = {}
+
+        def load(a):
+            if a < PAIRS:
+                raw = raw_pool.tile([P, x_pair], BF16)
+                nc.sync.dma_start(out=raw[:], in_=x_rows[:, a * x_pair : (a + 1) * x_pair])
+                raw_of[a] = raw
+
+        def transpose_pair(a):
+            if a < PAIRS:
+                x_words = raw_of[a][:].bitcast(F32)
+                tile_words = HEADS * UNIT_WORDS
+                x_grouped_of[a] = [
+                    transpose_units(x_words[:, i * tile_words : (i + 1) * tile_words], HEADS)
+                    for i in range(PAIR)
+                ]
+                x_quantised_of[a] = []
+                load(a + PAIRS_AHEAD)
+
+        def quantise_x(a, i):
+            if a < PAIRS:
+                x_codes = per_tile.tile([P, HEADS * UNIT_CODES], U32, align_bytes=64)
+                x_scales = per_tile.tile([P, HEADS * UNIT_CODES], U8, align_bytes=64)
+                quantise(x_grouped_of[a][i], x_codes[:], x_scales[:])
+                x_quantised_of[a].append((x_codes, x_scales))
+
+        def stage_1(a, i):
+            if 0 <= a < PAIRS:
+                if i == 0:
+                    o_grouped = per_pair.tile([P, PAIR * P * PACK], BF16, align_bytes=64)
+                    o_grouped_of[a] = o_grouped
+                x_codes, x_scales = x_quantised_of[a][i]
+                o_bank = banks.tile([P, PACK * P], F32, tag="bank")
+                for j in range(PACK):
+                    h = j // 2
+                    for g in range(PASSES):
+                        w_cols = slice((j * PASSES + g) * P, (j * PASSES + g + 1) * P)
+                        x_cols = slice((h * PASSES + g) * P, (h * PASSES + g + 1) * P)
+                        nc.tensor.matmul_mx(
+                            out=o_bank[:, j * P : (j + 1) * P],
+                            lhsT=w_codes[:, w_cols].bitcast(FP8X4),
+                            lhsT_scale=w_scales[:, w_cols],
+                            rhs=x_codes[:, x_cols].bitcast(FP8X4),
+                            rhs_scale=x_scales[:, x_cols],
+                            start=(g == 0),
+                            stop=(g == PASSES - 1),
+                        )
+                nc.vector.tensor_copy(
+                    out=o_grouped_of[a][:, i * P * PACK : (i + 1) * P * PACK].rearrange(
+                        "p (r j) -> p r j", j=PACK
+                    ),
+                    in_=o_bank[:].rearrange("p (j r) -> p r j", j=PACK),
+                )
+
+        def quantise_o(a):
+            if 0 <= a < PAIRS:
+                o_codes = per_pair.tile([P, PAIR * P], U32, align_bytes=64)
+                o_scales = per_pair.tile([P, PAIR * P], U8, align_bytes=64)
+                quantise(o_grouped_of[a], o_codes[:], o_scales[:])
+                o_quantised_of[a] = (o_codes, o_scales)
+
+        def stage_2(a):
+            if 0 <= a < PAIRS:
+                o_codes, o_scales = o_quantised_of[a]
+                out_bank = banks.tile([P, out_pair], F32, tag="bank")
+                for i in range(PAIR):
+                    nc.tensor.matmul_mx(
+                        out=out_bank[:, i * DIM : (i + 1) * DIM],
+                        lhsT=o_codes[:, i * P : (i + 1) * P].bitcast(FP8X4),
+                        lhsT_scale=o_scales[:, i * P : (i + 1) * P],
+                        rhs=wo_codes[:].bitcast(FP8X4),
+                        rhs_scale=wo_scales[:],
+                        start=True,
+                        stop=True,
+                    )
+                result = per_pair.tile([P, out_pair], F32)
+                nc.scalar.copy(out=result[:], in_=out_bank[:])
+                nc.sync.dma_start(out=out_rows[:, a * out_pair : (a + 1) * out_pair], in_=result[:])
+
         w_raw = keep.tile([P, HEADS * 2 * UNIT], BF16)
         nc.sync.dma_start(
             out=w_raw[:].rearrange("q (h f) -> q h f", h=HEADS),
             in_=w_uv.rearrange("h (q e) c -> q h (e c)", e=2),
         )
+        for a in range(RUN_PAIRS):
+            load(a)
         wo_raw = keep.tile([P, UNIT], BF16)
         nc.sync.dma_start(
             out=wo_raw[:].rearrange("p (a k) -> p a k", a=DIM // P),
             in_=wo.rearrange("(a p) k -> p a k", p=P),
         )
-        raw_of = {}
-        for r in range(ROUNDS_AHEAD):
-            raw_of[r] = load_round(r)
+        for a in range(RUN_PAIRS, PAIRS_AHEAD):
+            load(a)
 
         w_codes = keep.tile([P, HEADS * 2 * UNIT_CODES], U32, align_bytes=64)
         w_scales = keep.tile([P, HEADS * 2 * UNIT_CODES], U8, align_bytes=64)
-        wo_codes = keep.tile([P, DIM], U32, align_bytes=64)
-        wo_scales = keep.tile([P, DIM], U8, align_bytes=64)
         w_words = w_raw[:].bitcast(F32)
         for h in range(HEADS):
             w_grouped = transpose_units(w_words[:, h * 2 * UNIT_WORDS : (h + 1) * 2 * UNIT_WORDS], 2)
             head_cols = slice(h * 2 * UNIT_CODES, (h + 1) * 2 * UNIT_CODES)
             quantise(w_grouped, w_codes[:, head_cols], w_scales[:, head_cols])
-        wo_grouped = transpose_units(wo_raw[:].bitcast(F32), 1)
-        quantise(wo_grouped, wo_codes[:], wo_scales[:])
+        wo_codes = keep.tile([P, DIM], U32, align_bytes=64)
+        wo_scales = keep.tile([P, DIM], U8, align_bytes=64)
 
-        def stage_1(x_codes, x_scales, o_grouped_tile):
-            o_bank = o_banks.tile([P, PACK * P], F32)
-            for j in range(PACK):
-                h = j // 2
-                for g in range(PASSES):
-                    w_cols = slice((j * PASSES + g) * P, (j * PASSES + g + 1) * P)
-                    x_cols = slice((h * PASSES + g) * P, (h * PASSES + g + 1) * P)
-                    nc.tensor.matmul_mx(
-                        out=o_bank[:, j * P : (j + 1) * P],
-                        lhsT=w_codes[:, w_cols].bitcast(FP8X4),
-                        lhsT_scale=w_scales[:, w_cols],
-                        rhs=x_codes[:, x_cols].bitcast(FP8X4),
-                        rhs_scale=x_scales[:, x_cols],
-                        start=(g == 0),
-                        stop=(g == PASSES - 1),
-                    )
-            nc.vector.tensor_copy(
-                out=o_grouped_tile.rearrange("p (r j) -> p r j", j=PACK),
-                in_=o_bank[:].rearrange("p (j r) -> p r j", j=PACK),
-            )
+        for n in range(RUNS + 2):
+            first = n * RUN_PAIRS
+            quantise_o(first - 3)
+            quantise_o(first - 2)
 
-        def stage_2(r, o_codes, o_scales):
-            out_bank = out_banks.tile([P, out_round], F32)
-            for i in range(ROUND_TILES):
-                nc.tensor.matmul_mx(
-                    out=out_bank[:, i * DIM : (i + 1) * DIM],
-                    lhsT=o_codes[:, i * P : (i + 1) * P].bitcast(FP8X4),
-                    lhsT_scale=o_scales[:, i * P : (i + 1) * P],
-                    rhs=wo_codes[:].bitcast(FP8X4),
-                    rhs_scale=wo_scales[:],
-                    start=True,
-                    stop=True,
-                )
-            result = result_pool.tile([P, out_round], F32)
-            nc.scalar.copy(out=result[:], in_=out_bank[:])
-            nc.sync.dma_start(out=out_rows[:, r * out_round : (r + 1) * out_round], in_=result[:])
+            transpose_pair(first)
+            transpose_pair(first + 1)
+            if n == 0:
+                wo_grouped = transpose_units(wo_raw[:].bitcast(F32), 1)
 
-        x_quantised = {}
-        o_grouped_of = {}
-        for r in range(ROUNDS + 2):
-            transposing = r < ROUNDS
-            in_stage_1 = 0 <= r - 1 < ROUNDS
-            in_stage_2 = 0 <= r - 2
-
-            if in_stage_2:
-                o_codes = per_round.tile([P, ROUND_TILES * P], U32, align_bytes=64)
-                o_scales = per_round.tile([P, ROUND_TILES * P], U8, align_bytes=64)
-                quantise(o_grouped_of[r - 2], o_codes[:], o_scales[:])
-
-            if transposing:
-                x_words = raw_of[r][:].bitcast(F32)
-                tile_words = HEADS * UNIT_WORDS
-                x_grouped = [
-                    transpose_units(x_words[:, i * tile_words : (i + 1) * tile_words], HEADS)
-                    for i in range(ROUND_TILES)
-                ]
-                if r + ROUNDS_AHEAD < ROUNDS:
-                    raw_of[r + ROUNDS_AHEAD] = load_round(r + ROUNDS_AHEAD)
-                x_quantised[r] = []
-            if in_stage_1:
-                o_grouped = per_round.tile([P, ROUND_TILES * P * PACK], BF16, align_bytes=64)
-                o_grouped_of[r - 1] = o_grouped
-
-            for i in range(ROUND_TILES):
-                if transposing:
-                    x_codes = per_tile.tile([P, HEADS * UNIT_CODES], U32, align_bytes=64)
-                    x_scales = per_tile.tile([P, HEADS * UNIT_CODES], U8, align_bytes=64)
-                    quantise(x_grouped[i], x_codes[:], x_scales[:])
-                    x_quantised[r].append((x_codes, x_scales))
-                if in_stage_1:
-                    codes, scales = x_quantised[r - 1][i]
-                    stage_1(codes, scales, o_grouped[:, i * P * PACK : (i + 1) * P * PACK])
-
-            if in_stage_2:
-                stage_2(r - 2, o_codes, o_scales)
+            for i in range(PAIR):
+                quantise_x(first, i)
+            for i in range(PAIR):
+                stage_1(first - 1, i)
+            stage_2(first - 3)
+            stage_2(first - 2)
+            for i in range(PAIR):
+                quantise_x(first + 1, i)
+                stage_1(first, i)
+            if n == 0:
+                quantise(wo_grouped, wo_codes[:], wo_scales[:])

@@ -25,11 +25,10 @@ BLOCKS = UNIT_WORDS // P
 PASSES = LATENT // (P * PACK)
 PSUM_BANKS = 8
 
-PAIR = 2
-PAIRS = TOKENS // (P * PAIR)
-RUN_PAIRS = 2
-RUNS = PAIRS // RUN_PAIRS
-PAIRS_AHEAD = 6
+TILES = TOKENS // P
+RUN = 4
+LAG = RUN // 2
+TILES_AHEAD = 3 * RUN
 
 FLOPS = 2 * TOKENS * HEADS * V_HEAD * LATENT + 2 * TOKENS * JOINED * DIM
 
@@ -37,16 +36,13 @@ FLOPS = 2 * TOKENS * HEADS * V_HEAD * LATENT + 2 * TOKENS * JOINED * DIM
 def tile_mla_pc_t_kernel(tc, o_lat, w_uv, wo, out):
     nc = tc.nc
 
-    x_rows = o_lat.rearrange("b (q t) h c -> (b q) (t h c)", t=PAIR * PAIRS)
-    out_rows = out.rearrange("b (q t) f -> (b q) (t f)", t=PAIR * PAIRS)
-    x_pair = PAIR * HEADS * LATENT
-    out_pair = PAIR * DIM
+    x_rows = o_lat.rearrange("b (q t) h c -> (b q) t (h c)", t=TILES)
+    out_rows = out.rearrange("b (q t) f -> (b q) t f", t=TILES)
 
     with ExitStack() as ctx:
         keep = ctx.enter_context(tc.tile_pool(name="keep", bufs=1))
-        raw_pool = ctx.enter_context(tc.tile_pool(name="raw", bufs=PAIRS_AHEAD))
-        per_tile = ctx.enter_context(tc.tile_pool(name="per_tile", bufs=2 * RUN_PAIRS * PAIR))
-        per_pair = ctx.enter_context(tc.tile_pool(name="per_pair", bufs=2 * RUN_PAIRS))
+        raw_pool = ctx.enter_context(tc.tile_pool(name="raw", bufs=TILES_AHEAD))
+        per_tile = ctx.enter_context(tc.tile_pool(name="per_tile", bufs=2 * RUN))
         banks = ctx.enter_context(tc.psum_pool(name="banks", bufs=PSUM_BANKS))
         ctx.enter_context(tc.manual_schedule())
 
@@ -81,36 +77,27 @@ def tile_mla_pc_t_kernel(tc, o_lat, w_uv, wo, out):
         o_grouped_of = {}
         o_quantised_of = {}
 
-        def load(a):
-            if a < PAIRS:
-                raw = raw_pool.tile([P, x_pair], BF16)
-                nc.sync.dma_start(out=raw[:], in_=x_rows[:, a * x_pair : (a + 1) * x_pair])
-                raw_of[a] = raw
+        def load(t):
+            if t < TILES:
+                raw = raw_pool.tile([P, HEADS * LATENT], BF16)
+                nc.sync.dma_start(out=raw[:], in_=x_rows[:, t, :])
+                raw_of[t] = raw
 
-        def transpose_pair(a):
-            if a < PAIRS:
-                x_words = raw_of[a][:].bitcast(F32)
-                tile_words = HEADS * UNIT_WORDS
-                x_grouped_of[a] = [
-                    transpose_units(x_words[:, i * tile_words : (i + 1) * tile_words], HEADS)
-                    for i in range(PAIR)
-                ]
-                x_quantised_of[a] = []
-                load(a + PAIRS_AHEAD)
+        def transpose_tile(t):
+            if t < TILES:
+                x_grouped_of[t] = transpose_units(raw_of[t][:].bitcast(F32), HEADS)
+                load(t + TILES_AHEAD)
 
-        def quantise_x(a, i):
-            if a < PAIRS:
+        def quantise_x(t):
+            if t < TILES:
                 x_codes = per_tile.tile([P, HEADS * UNIT_CODES], U32, align_bytes=64)
                 x_scales = per_tile.tile([P, HEADS * UNIT_CODES], U8, align_bytes=64)
-                quantise(x_grouped_of[a][i], x_codes[:], x_scales[:])
-                x_quantised_of[a].append((x_codes, x_scales))
+                quantise(x_grouped_of[t], x_codes[:], x_scales[:])
+                x_quantised_of[t] = (x_codes, x_scales)
 
-        def stage_1(a, i):
-            if 0 <= a < PAIRS:
-                if i == 0:
-                    o_grouped = per_pair.tile([P, PAIR * P * PACK], BF16, align_bytes=64)
-                    o_grouped_of[a] = o_grouped
-                x_codes, x_scales = x_quantised_of[a][i]
+        def stage_1(t):
+            if 0 <= t < TILES:
+                x_codes, x_scales = x_quantised_of[t]
                 o_bank = banks.tile([P, PACK * P], F32, tag="bank")
                 for j in range(PACK):
                     h = j // 2
@@ -126,52 +113,48 @@ def tile_mla_pc_t_kernel(tc, o_lat, w_uv, wo, out):
                             start=(g == 0),
                             stop=(g == PASSES - 1),
                         )
+                o_grouped = per_tile.tile([P, P * PACK], BF16, align_bytes=64)
                 nc.vector.tensor_copy(
-                    out=o_grouped_of[a][:, i * P * PACK : (i + 1) * P * PACK].rearrange(
-                        "p (r j) -> p r j", j=PACK
-                    ),
+                    out=o_grouped[:].rearrange("p (r j) -> p r j", j=PACK),
                     in_=o_bank[:].rearrange("p (j r) -> p r j", j=PACK),
                 )
+                o_grouped_of[t] = o_grouped
 
-        def quantise_o(a):
-            if 0 <= a < PAIRS:
-                o_codes = per_pair.tile([P, PAIR * P], U32, align_bytes=64)
-                o_scales = per_pair.tile([P, PAIR * P], U8, align_bytes=64)
-                quantise(o_grouped_of[a], o_codes[:], o_scales[:])
-                o_quantised_of[a] = (o_codes, o_scales)
+        def quantise_o(t):
+            if 0 <= t < TILES:
+                o_codes = per_tile.tile([P, P], U32, align_bytes=64)
+                o_scales = per_tile.tile([P, P], U8, align_bytes=64)
+                quantise(o_grouped_of[t], o_codes[:], o_scales[:])
+                o_quantised_of[t] = (o_codes, o_scales)
 
-        def stage_2(a):
-            if 0 <= a < PAIRS:
-                o_codes, o_scales = o_quantised_of[a]
-                out_bank = banks.tile([P, out_pair], F32, tag="bank")
-                for i in range(PAIR):
-                    nc.tensor.matmul_mx(
-                        out=out_bank[:, i * DIM : (i + 1) * DIM],
-                        lhsT=o_codes[:, i * P : (i + 1) * P].bitcast(FP8X4),
-                        lhsT_scale=o_scales[:, i * P : (i + 1) * P],
-                        rhs=wo_codes[:].bitcast(FP8X4),
-                        rhs_scale=wo_scales[:],
-                        start=True,
-                        stop=True,
-                    )
-                result = per_pair.tile([P, out_pair], F32)
+        def stage_2(t):
+            if 0 <= t < TILES:
+                o_codes, o_scales = o_quantised_of[t]
+                out_bank = banks.tile([P, DIM], F32, tag="bank")
+                nc.tensor.matmul_mx(
+                    out=out_bank[:],
+                    lhsT=o_codes[:].bitcast(FP8X4),
+                    lhsT_scale=o_scales[:],
+                    rhs=wo_codes[:].bitcast(FP8X4),
+                    rhs_scale=wo_scales[:],
+                    start=True,
+                    stop=True,
+                )
+                result = per_tile.tile([P, DIM], F32)
                 nc.scalar.copy(out=result[:], in_=out_bank[:])
-                nc.sync.dma_start(out=out_rows[:, a * out_pair : (a + 1) * out_pair], in_=result[:])
+                nc.sync.dma_start(out=out_rows[:, t, :], in_=result[:])
 
         w_raw = keep.tile([P, HEADS * 2 * UNIT], BF16)
-        nc.sync.dma_start(
-            out=w_raw[:].rearrange("q (h f) -> q h f", h=HEADS),
-            in_=w_uv.rearrange("h (q e) c -> q h (e c)", e=2),
-        )
-        for a in range(RUN_PAIRS):
-            load(a)
+        w_rows = w_uv.rearrange("h (q e) c -> q h (e c)", e=2)
+        for h in range(HEADS):
+            nc.sync.dma_start(out=w_raw[:, h * 2 * UNIT : (h + 1) * 2 * UNIT], in_=w_rows[:, h, :])
         wo_raw = keep.tile([P, UNIT], BF16)
         nc.sync.dma_start(
             out=wo_raw[:].rearrange("p (a k) -> p a k", a=DIM // P),
             in_=wo.rearrange("(a p) k -> p a k", p=P),
         )
-        for a in range(RUN_PAIRS, PAIRS_AHEAD):
-            load(a)
+        for t in range(TILES_AHEAD):
+            load(t)
 
         w_codes = keep.tile([P, HEADS * 2 * UNIT_CODES], U32, align_bytes=64)
         w_scales = keep.tile([P, HEADS * 2 * UNIT_CODES], U8, align_bytes=64)
@@ -182,25 +165,34 @@ def tile_mla_pc_t_kernel(tc, o_lat, w_uv, wo, out):
             quantise(w_grouped, w_codes[:, head_cols], w_scales[:, head_cols])
         wo_codes = keep.tile([P, DIM], U32, align_bytes=64)
         wo_scales = keep.tile([P, DIM], U8, align_bytes=64)
+        wo_grouped = transpose_units(wo_raw[:].bitcast(F32), 1)
+        quantise(wo_grouped, wo_codes[:], wo_scales[:])
 
-        for n in range(RUNS + 2):
-            first = n * RUN_PAIRS
-            quantise_o(first - 3)
-            quantise_o(first - 2)
+        lengths = [1] * RUN + [RUN] * (TILES // RUN - 1) + [RUN] * 2
+        first = 0
+        in_stage_2 = range(0)
+        for length in lengths:
+            transposed = range(first, first + length)
+            in_stage_1 = range(first - LAG, first + length - LAG)
+            old = [t for t in in_stage_1 if t < first]
+            new = [t for t in in_stage_1 if t >= first]
 
-            transpose_pair(first)
-            transpose_pair(first + 1)
-            if n == 0:
-                wo_grouped = transpose_units(wo_raw[:].bitcast(F32), 1)
+            for t in in_stage_2:
+                quantise_o(t)
+            for t in transposed:
+                transpose_tile(t)
 
-            for i in range(PAIR):
-                quantise_x(first, i)
-            for i in range(PAIR):
-                stage_1(first - 1, i)
-            stage_2(first - 3)
-            stage_2(first - 2)
-            for i in range(PAIR):
-                quantise_x(first + 1, i)
-                stage_1(first, i)
-            if n == 0:
-                quantise(wo_grouped, wo_codes[:], wo_scales[:])
+            for t in new:
+                quantise_x(t)
+            for t in old:
+                stage_1(t)
+            for t in in_stage_2:
+                stage_2(t)
+            for t in transposed:
+                if t not in new:
+                    quantise_x(t)
+            for t in new:
+                stage_1(t)
+
+            in_stage_2 = in_stage_1
+            first += length

from contextlib import ExitStack

import concourse.masks as masks
import concourse.mybir as mybir

F32 = mybir.dt.float32
BF16 = mybir.dt.bfloat16
U32 = mybir.dt.uint32
U8 = mybir.dt.uint8
FP8X4 = mybir.dt.float8_e4m3fn_x4

P = 128
TOKENS = 4 * 1024
HEADS = 2
LATENT = 1024
V_HEAD = 256
JOINED = HEADS * V_HEAD
DIM = 256

PACK = 4
UNIT = 1024
UNIT_WORDS = UNIT // 2
UNIT_CODES = UNIT // PACK
BLOCKS = UNIT_WORDS // P
PASSES = LATENT // (P * PACK)
PSUM_BANKS = 8

TILES = TOKENS // P
RUN = 4
LAG = RUN // 2
TILES_AHEAD = 3 * RUN

FLOPS = 2 * TOKENS * HEADS * V_HEAD * LATENT + 2 * TOKENS * JOINED * DIM


def tile_mla_pc_t_kernel(tc, o_lat, w_uv, wo, out):
    nc = tc.nc

    x_rows = o_lat.rearrange("b (q t) h c -> (b q) t (h c)", t=TILES)
    out_rows = out.rearrange("b (q t) f -> (b q) t f", t=TILES)

    with ExitStack() as ctx:
        keep = ctx.enter_context(tc.tile_pool(name="keep", bufs=1))
        raw_pool = ctx.enter_context(tc.tile_pool(name="raw", bufs=TILES_AHEAD))
        per_tile = ctx.enter_context(tc.tile_pool(name="per_tile", bufs=2 * RUN))
        banks = ctx.enter_context(tc.psum_pool(name="banks", bufs=PSUM_BANKS))
        ctx.enter_context(tc.manual_schedule())

        identity = keep.tile([P, P], F32)
        masks.make_identity(nc, identity[:])

        def transpose_units(words, units):
            grouped = per_tile.tile([P, units * UNIT], BF16, tag="grouped", align_bytes=64)
            grouped_words = grouped[:].bitcast(F32)
            for n in range(units):
                bank = banks.tile([P, UNIT_WORDS], F32, tag="bank")
                for block in range(BLOCKS):
                    nc.tensor.transpose(
                        bank[:, block * P : (block + 1) * P],
                        words[:, n * UNIT_WORDS + block * P : n * UNIT_WORDS + (block + 1) * P],
                        identity[:],
                    )
                nc.scalar.copy(
                    out=grouped_words[:, n * UNIT_WORDS : (n + 1) * UNIT_WORDS].rearrange(
                        "p (g r u) -> p g r u", g=PASSES, u=2
                    ),
                    in_=bank[:].rearrange("p (g u r) -> p g r u", g=PASSES, u=2),
                )
            return grouped

        def quantise(grouped, codes, scales):
            nc.vector.quantize_mx(out=codes.bitcast(FP8X4), scales=scales, in_=grouped[:])

        raw_of = {}
        x_grouped_of = {}
        x_quantised_of = {}
        o_grouped_of = {}
        o_quantised_of = {}

        def load(t):
            if t < TILES:
                raw = raw_pool.tile([P, HEADS * LATENT], BF16)
                nc.sync.dma_start(out=raw[:], in_=x_rows[:, t, :])
                raw_of[t] = raw

        def transpose_tile(t):
            if t < TILES:
                x_grouped_of[t] = transpose_units(raw_of[t][:].bitcast(F32), HEADS)
                load(t + TILES_AHEAD)

        def quantise_x(t):
            if t < TILES:
                x_codes = per_tile.tile([P, HEADS * UNIT_CODES], U32, align_bytes=64)
                x_scales = per_tile.tile([P, HEADS * UNIT_CODES], U8, align_bytes=64)
                quantise(x_grouped_of[t], x_codes[:], x_scales[:])
                x_quantised_of[t] = (x_codes, x_scales)

        def stage_1(t):
            if 0 <= t < TILES:
                x_codes, x_scales = x_quantised_of[t]
                o_bank = banks.tile([P, PACK * P], F32, tag="bank")
                for j in range(PACK):
                    h = j // 2
                    for g in range(PASSES):
                        w_cols = slice((j * PASSES + g) * P, (j * PASSES + g + 1) * P)
                        x_cols = slice((h * PASSES + g) * P, (h * PASSES + g + 1) * P)
                        nc.tensor.matmul_mx(
                            out=o_bank[:, j * P : (j + 1) * P],
                            lhsT=w_codes[:, w_cols].bitcast(FP8X4),
                            lhsT_scale=w_scales[:, w_cols],
                            rhs=x_codes[:, x_cols].bitcast(FP8X4),
                            rhs_scale=x_scales[:, x_cols],
                            start=(g == 0),
                            stop=(g == PASSES - 1),
                        )
                o_grouped = per_tile.tile([P, P * PACK], BF16, align_bytes=64)
                nc.vector.tensor_copy(
                    out=o_grouped[:].rearrange("p (r j) -> p r j", j=PACK),
                    in_=o_bank[:].rearrange("p (j r) -> p r j", j=PACK),
                )
                o_grouped_of[t] = o_grouped

        def quantise_o(t):
            if 0 <= t < TILES:
                o_codes = per_tile.tile([P, P], U32, align_bytes=64)
                o_scales = per_tile.tile([P, P], U8, align_bytes=64)
                quantise(o_grouped_of[t], o_codes[:], o_scales[:])
                o_quantised_of[t] = (o_codes, o_scales)

        def stage_2(t):
            if 0 <= t < TILES:
                o_codes, o_scales = o_quantised_of[t]
                out_bank = banks.tile([P, DIM], F32, tag="bank")
                nc.tensor.matmul_mx(
                    out=out_bank[:],
                    lhsT=o_codes[:].bitcast(FP8X4),
                    lhsT_scale=o_scales[:],
                    rhs=wo_codes[:].bitcast(FP8X4),
                    rhs_scale=wo_scales[:],
                    start=True,
                    stop=True,
                )
                result = per_tile.tile([P, DIM], F32)
                nc.scalar.copy(out=result[:], in_=out_bank[:])
                nc.sync.dma_start(out=out_rows[:, t, :], in_=result[:])

        w_raw = keep.tile([P, HEADS * 2 * UNIT], BF16)
        w_rows = w_uv.rearrange("h (q e) c -> q h (e c)", e=2)
        for h in range(HEADS):
            nc.sync.dma_start(out=w_raw[:, h * 2 * UNIT : (h + 1) * 2 * UNIT], in_=w_rows[:, h, :])
        wo_raw = keep.tile([P, UNIT], BF16)
        nc.sync.dma_start(
            out=wo_raw[:].rearrange("p (a k) -> p a k", a=DIM // P),
            in_=wo.rearrange("(a p) k -> p a k", p=P),
        )
        for t in range(TILES_AHEAD):
            load(t)

        w_codes = keep.tile([P, HEADS * 2 * UNIT_CODES], U32, align_bytes=64)
        w_scales = keep.tile([P, HEADS * 2 * UNIT_CODES], U8, align_bytes=64)
        w_words = w_raw[:].bitcast(F32)
        for h in range(HEADS):
            w_grouped = transpose_units(w_words[:, h * 2 * UNIT_WORDS : (h + 1) * 2 * UNIT_WORDS], 2)
            head_cols = slice(h * 2 * UNIT_CODES, (h + 1) * 2 * UNIT_CODES)
            quantise(w_grouped, w_codes[:, head_cols], w_scales[:, head_cols])
        wo_codes = keep.tile([P, DIM], U32, align_bytes=64)
        wo_scales = keep.tile([P, DIM], U8, align_bytes=64)
        wo_grouped = transpose_units(wo_raw[:].bitcast(F32), 1)
        quantise(wo_grouped, wo_codes[:], wo_scales[:])

        lengths = [1] * RUN + [RUN] * (TILES // RUN - 1) + [RUN] * 2
        first = 0
        in_stage_2 = range(0)
        for length in lengths:
            transposed = range(first, first + length)
            in_stage_1 = range(first - LAG, first + length - LAG)
            old = [t for t in in_stage_1 if t < first]
            new = [t for t in in_stage_1 if t >= first]

            for t in in_stage_2:
                quantise_o(t)
            for t in transposed:
                transpose_tile(t)

            for t in new:
                quantise_x(t)
            for t in old:
                stage_1(t)
            for t in in_stage_2:
                stage_2(t)
            for t in transposed:
                if t not in new:
                    quantise_x(t)
            for t in new:
                stage_1(t)

            in_stage_2 = in_stage_1
            first += length
